import numpy as np
import ml_dtypes


def mxq(x, axis, fmt="e4m3"):
    dtype, down = {"e4m3": (ml_dtypes.float8_e4m3fn, 7), "e5m2": (ml_dtypes.float8_e5m2, 14)}[fmt]
    v = np.moveaxis(np.asarray(x, np.float32).astype(ml_dtypes.bfloat16).astype(np.float64), axis, -1)
    blocks = v.reshape(v.shape[:-1] + (-1, 32))
    amax = np.abs(blocks).max(-1, keepdims=True)
    byte = np.maximum(np.where(amax > 0, np.frexp(amax)[1] - 1 + 127, 0) - down, 1)
    scale = np.exp2(byte - 127.0)
    codes = (blocks / scale).astype(np.float32).astype(dtype).astype(np.float64)
    return np.moveaxis((codes * scale).reshape(v.shape), -1, axis)


WIDE = False


def mx_kscale(k):
    if not WIDE:
        return np.ones(k)
    levels = np.array([10, -10, 5, -5, 0])
    if k % 512:
        return np.exp2(np.random.permutation(np.resize(levels, k // 32))).repeat(32)
    a = np.empty((k // 512, 16))
    for p in range(k // 512):
        a[p, :8] = np.random.permutation(np.resize(levels, 8))
        for g in range(8):
            far = levels[np.abs(levels - a[p, g]) >= 10]
            a[p, g + 8] = far[np.random.randint(len(far))]
    return np.exp2(a.ravel()).repeat(32)


BF16 = ml_dtypes.bfloat16


def bf(x):
    return np.asarray(x, np.float32).astype(BF16)


def f64(x):
    return np.asarray(x).astype(np.float64)


N, C, P, D = 512, 128, 7, 1024
SCALE = 1.0 / np.sqrt(D)


def setup_inputs():
    s, t = mx_kscale(D), mx_kscale(D)
    return {"h": bf(np.random.standard_normal((N, D)) * s),
            "w_q": bf(np.random.standard_normal((D, D)) * 1.6 / np.sqrt(D) / s * t[:, None]),
            "b_q": bf(np.random.standard_normal(D) * 0.2 * t),
            "w_k": bf(np.random.standard_normal((D, D)) * 1.6 / np.sqrt(D) / s / t[:, None]),
            "b_k": bf(np.random.standard_normal(D) * 0.2 / t)}


def reference(h, w_q, b_q, w_k, b_k):
    hq = mxq(f64(h), 1, "e4m3")
    q = (hq @ mxq(f64(w_q).T, 0, "e4m3")) + f64(b_q)
    k = (hq @ mxq(f64(w_k).T, 0, "e4m3")) + f64(b_k)
    return (mxq(q, 1, "e4m3") @ mxq(k.T, 0, "e4m3")) * SCALE

@@ -1,0 +1,216 @@
+from contextlib import ExitStack
+import math
+
+import concourse.mybir as mybir
+from concourse.masks import make_identity
+
+F32 = mybir.dt.float32
+BF16 = mybir.dt.bfloat16
+U32 = mybir.dt.uint32
+U8 = mybir.dt.uint8
+FP8X4 = mybir.dt.float8_e4m3fn_x4
+
+P = 128
+PACK = 4
+K_PASS = P * PACK
+PROPOSALS = 512
+FEATURES = 1024
+PASSES = FEATURES // K_PASS
+GROUPS = PROPOSALS // P
+PAIRS = FEATURES // 2
+PAIRS_IN_WORD = PACK // 2
+TILE_WORDS = PASSES * P
+LOAD_ROWS = 2
+LOADS = PACK // LOAD_ROWS
+FIRST_LEAD = 2
+PSUM_BANKS = 8
+MX_ALIGN = 64
+SCALE = 1.0 / math.sqrt(FEATURES)
+
+FLOPS = 2 * 2 * PROPOSALS * FEATURES * FEATURES + 2 * PROPOSALS * PROPOSALS * FEATURES
+
+
+def transpose_rows(nc, banks, keep, raw, identity, label):
+    count = raw[:].shape[1]
+    grouped = keep.tile([P, count * FEATURES], BF16, name="grouped_" + label, align_bytes=MX_ALIGN)
+    for c in range(count):
+        pairs = raw[:, c, :].bitcast(F32)
+        turned = banks.tile([P, PAIRS], F32, tag="bank")
+        for g in range(PASSES):
+            for u in range(PAIRS_IN_WORD):
+                block = PAIRS_IN_WORD * g + u
+                first = g * PAIRS_IN_WORD * P + u
+                nc.tensor.transpose(
+                    turned[:, block * P : (block + 1) * P],
+                    pairs[:, first : (g + 1) * PAIRS_IN_WORD * P : PAIRS_IN_WORD],
+                    identity[:],
+                )
+        nc.scalar.copy(
+            out=grouped[:, c * FEATURES : (c + 1) * FEATURES]
+            .bitcast(F32)
+            .rearrange("p (g r u) -> p g r u", g=PASSES, u=PAIRS_IN_WORD),
+            in_=turned[:].rearrange("p (g u r) -> p g r u", g=PASSES, u=PAIRS_IN_WORD),
+        )
+    return grouped
+
+
+def quantise_rows(nc, keep, grouped, label):
+    width = grouped[:].shape[1] // PACK
+    codes = keep.tile([P, width], U32, name="codes_" + label, align_bytes=MX_ALIGN)
+    scales = keep.tile([P, width], U8, name="scales_" + label, align_bytes=MX_ALIGN)
+    nc.vector.quantize_mx(out=codes[:].bitcast(FP8X4), scales=scales[:], in_=grouped[:])
+    return [
+        (codes[:, first : first + TILE_WORDS], scales[:, first : first + TILE_WORDS])
+        for first in range(0, width, TILE_WORDS)
+    ]
+
+
+def project(nc, sums_pool, weights, proposals):
+    sums = sums_pool.tile([P, PACK, P], F32, tag="sums")
+    h_codes, h_scales = proposals
+    for t in range(PACK):
+        w_codes, w_scales = weights[t]
+        for g in range(PASSES):
+            cols = slice(g * P, (g + 1) * P)
+            nc.tensor.matmul_mx(
+                out=sums[:, t, :],
+                lhsT=w_codes[:, cols].bitcast(FP8X4),
+                lhsT_scale=w_scales[:, cols],
+                rhs=h_codes[:, cols].bitcast(FP8X4),
+                rhs_scale=h_scales[:, cols],
+                start=(g == 0),
+                stop=(g == PASSES - 1),
+            )
+    return sums
+
+
+def tile_selsahead_pb_kernel(tc, h, w_q, b_q, w_k, b_k, out):
+    nc = tc.nc
+    weight_dram = {"q": w_q, "k": w_k}
+    bias_dram = {"q": b_q, "k": b_k}
+    quarters = [("k", 0), ("q", 0), ("k", 1), ("q", 1)]
+
+    with ExitStack() as ctx:
+        ctx.enter_context(tc.manual_schedule())
+        keep = ctx.enter_context(tc.tile_pool(name="keep", bufs=1))
+        banks = ctx.enter_context(tc.psum_pool(name="banks", bufs=PSUM_BANKS // 2))
+        sums_pool = ctx.enter_context(tc.psum_pool(name="sums", bufs=PSUM_BANKS // 2))
+
+        identity = keep.tile([P, P], F32, name="identity")
+        make_identity(nc, identity[:])
+
+        bias = {}
+        for m in ("k", "q"):
+            bias[m] = keep.tile([P, PASSES, PACK], BF16, name="bias_" + m)
+            nc.scalar.dma_start(
+                out=bias[m][:],
+                in_=bias_dram[m].rearrange("(g p t) -> p g t", g=PASSES, p=P, t=PACK),
+            )
+
+        def load_quarter(m, f_pass):
+            rows = weight_dram[m].rearrange("(g p t) d -> g p t d", g=PASSES, p=P, t=PACK)
+            loaded = []
+            for j in range(LOADS):
+                raw = keep.tile([P, LOAD_ROWS, FEATURES], BF16, name="raw_%s%d_%d" % (m, f_pass, j))
+                nc.sync.dma_start(
+                    out=raw[:], in_=rows[f_pass, :, j * LOAD_ROWS : (j + 1) * LOAD_ROWS, :]
+                )
+                loaded.append(raw)
+            return loaded
+
+        w_raw = {quarters[0]: load_quarter(*quarters[0])}
+        h_raw = []
+        for i in range(GROUPS):
+            raw = keep.tile([P, 1, FEATURES], BF16, name="raw_h%d" % i)
+            nc.sync.dma_start(out=raw[:, 0, :], in_=h[i * P : (i + 1) * P, :])
+            h_raw.append(raw)
+        for quarter in quarters[1:]:
+            w_raw[quarter] = load_quarter(*quarter)
+
+        qk_codes = {}
+        qk_scales = {}
+        for m, f_pass in quarters:
+            qk_codes[(m, f_pass)] = keep.tile(
+                [P, PROPOSALS], U32, name="codes_%s%d" % (m, f_pass), align_bytes=MX_ALIGN
+            )
+            qk_scales[(m, f_pass)] = keep.tile(
+                [P, PROPOSALS], U8, name="scales_%s%d" % (m, f_pass), align_bytes=MX_ALIGN
+            )
+
+        def transpose_quarter(quarter):
+            return [
+                transpose_rows(nc, banks, keep, w_raw[quarter][j], identity, "%s%d_%d" % (quarter + (j,)))
+                for j in range(LOADS)
+            ]
+
+        def quantise_load(quarter, quarter_grouped, j):
+            return quantise_rows(nc, keep, quarter_grouped[j], "%s%d_%d" % (quarter + (j,)))
+
+        def affinity_pass(logits_i, i, f_pass):
+            cols = slice(i * P, (i + 1) * P)
+            nc.tensor.matmul_mx(
+                out=logits_i[:],
+                lhsT=qk_codes[("q", f_pass)][:, cols].bitcast(FP8X4),
+                lhsT_scale=qk_scales[("q", f_pass)][:, cols],
+                rhs=qk_codes[("k", f_pass)][:].bitcast(FP8X4),
+                rhs_scale=qk_scales[("k", f_pass)][:],
+                start=(f_pass == 0),
+                stop=(f_pass == PASSES - 1),
+            )
+
+        next_grouped = transpose_quarter(quarters[0])
+        next_mx = []
+        for j in range(LOADS):
+            next_mx.extend(quantise_load(quarters[0], next_grouped, j))
+        h_mx = []
+        for i in range(GROUPS):
+            h_grouped = transpose_rows(nc, banks, keep, h_raw[i], identity, "h%d" % i)
+            h_mx.extend(quantise_rows(nc, keep, h_grouped, "h%d" % i))
+
+        logits = []
+        for step, (m, f_pass) in enumerate(quarters):
+            last = step == len(quarters) - 1
+            this_mx = next_mx
+            next_mx = []
+            lead = FIRST_LEAD if step == 0 else 0
+            products = [project(nc, sums_pool, this_mx, h_mx[i]) for i in range(lead)]
+            if last:
+                for i in range(GROUPS):
+                    logits.append(banks.tile([P, PROPOSALS], F32, tag="bank", name="logits_%d" % i))
+                    affinity_pass(logits[i], i, 0)
+            else:
+                next_grouped = transpose_quarter(quarters[step + 1])
+            products.extend([project(nc, sums_pool, this_mx, h_mx[i]) for i in range(lead, GROUPS)])
+
+            def finish_group(i):
+                cols = slice(i * P, (i + 1) * P)
+                nc.vector.quantize_mx(
+                    out=qk_codes[(m, f_pass)][:, cols].bitcast(FP8X4),
+                    scales=qk_scales[(m, f_pass)][:, cols],
+                    in_=rounded[i][:],
+                )
+                if last:
+                    affinity_pass(logits[i], i, 1)
+                    scaled = keep.tile([P, PROPOSALS], F32, name="scaled_%d" % i)
+                    nc.scalar.mul(out=scaled[:], in_=logits[i][:], mul=SCALE)
+                    nc.sync.dma_start(out=out[cols, :], in_=scaled[:])
+
+            rounded = []
+            for i in range(GROUPS):
+                j = i - lead
+                if not last and 0 <= j < LOADS:
+                    next_mx.extend(quantise_load(quarters[step + 1], next_grouped, j))
+                rounded.append(
+                    keep.tile(
+                        [P, P * PACK], BF16, name="rounded_%s%d_%d" % (m, f_pass, i), align_bytes=MX_ALIGN
+                    )
+                )
+                nc.vector.tensor_tensor(
+                    out=rounded[i][:].rearrange("p (n t) -> p n t", t=PACK),
+                    in0=products[i][:].rearrange("p t n -> p n t"),
+                    in1=bias[m][:, f_pass, :].unsqueeze(1).to_broadcast([P, P, PACK]),
+                    op=mybir.AluOpType.add,
+                )
+                if i >= 1:
+                    finish_group(i - 1)
+            finish_group(GROUPS - 1)

@@ -1,4 +1,5 @@
 from contextlib import ExitStack
+import functools
 import math
 
 import concourse.mybir as mybir
@@ -21,7 +22,8 @@ PAIRS = FEATURES // 2
 PAIRS_IN_WORD = PACK // 2
 TILE_WORDS = PASSES * P
 LOAD_ROWS = 2
-LOADS = PACK // LOAD_ROWS
+HEAD_LOAD_ROWS = 1
+SCALAR_GROUPS = {("k", 1): [1], ("q", 1): [1]}
 FIRST_LEAD = 2
 PSUM_BANKS = 8
 MX_ALIGN = 64
@@ -65,8 +67,8 @@ def quantise_rows(nc, keep, grouped, label):
     ]
 
 
-def project(nc, sums_pool, weights, proposals):
-    sums = sums_pool.tile([P, PACK, P], F32, tag="sums")
+def project(nc, banks, weights, proposals):
+    sums = banks.tile([P, PACK, P], F32, tag="bank")
     h_codes, h_scales = proposals
     for t in range(PACK):
         w_codes, w_scales = weights[t]
@@ -93,39 +95,39 @@ def tile_selsahead_pb_kernel(tc, h, w_q, b_q, w_k, b_k, out):
     with ExitStack() as ctx:
         ctx.enter_context(tc.manual_schedule())
         keep = ctx.enter_context(tc.tile_pool(name="keep", bufs=1))
-        banks = ctx.enter_context(tc.psum_pool(name="banks", bufs=PSUM_BANKS // 2))
-        sums_pool = ctx.enter_context(tc.psum_pool(name="sums", bufs=PSUM_BANKS // 2))
+        banks = ctx.enter_context(tc.psum_pool(name="banks", bufs=PSUM_BANKS))
 
         identity = keep.tile([P, P], F32, name="identity")
         make_identity(nc, identity[:])
 
         bias = {}
-        for m in ("k", "q"):
+
+        def load_bias(m):
             bias[m] = keep.tile([P, PASSES, PACK], BF16, name="bias_" + m)
-            nc.scalar.dma_start(
+            nc.sync.dma_start(
                 out=bias[m][:],
                 in_=bias_dram[m].rearrange("(g p t) -> p g t", g=PASSES, p=P, t=PACK),
             )
 
-        def load_quarter(m, f_pass):
+        def load_quarter(m, f_pass, load_rows):
             rows = weight_dram[m].rearrange("(g p t) d -> g p t d", g=PASSES, p=P, t=PACK)
             loaded = []
-            for j in range(LOADS):
-                raw = keep.tile([P, LOAD_ROWS, FEATURES], BF16, name="raw_%s%d_%d" % (m, f_pass, j))
-                nc.sync.dma_start(
-                    out=raw[:], in_=rows[f_pass, :, j * LOAD_ROWS : (j + 1) * LOAD_ROWS, :]
-                )
+            for first in range(0, PACK, load_rows):
+                raw = keep.tile([P, load_rows, FEATURES], BF16, name="raw_%s%d_%d" % (m, f_pass, first))
+                nc.sync.dma_start(out=raw[:], in_=rows[f_pass, :, first : first + load_rows, :])
                 loaded.append(raw)
             return loaded
 
-        w_raw = {quarters[0]: load_quarter(*quarters[0])}
+        w_raw = {quarters[0]: load_quarter(*quarters[0], HEAD_LOAD_ROWS)}
         h_raw = []
         for i in range(GROUPS):
             raw = keep.tile([P, 1, FEATURES], BF16, name="raw_h%d" % i)
             nc.sync.dma_start(out=raw[:, 0, :], in_=h[i * P : (i + 1) * P, :])
             h_raw.append(raw)
+        load_bias("k")
+        load_bias("q")
         for quarter in quarters[1:]:
-            w_raw[quarter] = load_quarter(*quarter)
+            w_raw[quarter] = load_quarter(*quarter, LOAD_ROWS)
 
         qk_codes = {}
         qk_scales = {}
@@ -139,8 +141,8 @@ def tile_selsahead_pb_kernel(tc, h, w_q, b_q, w_k, b_k, out):
 
         def transpose_quarter(quarter):
             return [
-                transpose_rows(nc, banks, keep, w_raw[quarter][j], identity, "%s%d_%d" % (quarter + (j,)))
-                for j in range(LOADS)
+                transpose_rows(nc, banks, keep, raw, identity, "%s%d_%d" % (quarter + (j,)))
+                for j, raw in enumerate(w_raw[quarter])
             ]
 
         def quantise_load(quarter, quarter_grouped, j):
@@ -160,7 +162,7 @@ def tile_selsahead_pb_kernel(tc, h, w_q, b_q, w_k, b_k, out):
 
         next_grouped = transpose_quarter(quarters[0])
         next_mx = []
-        for j in range(LOADS):
+        for j in range(len(next_grouped)):
             next_mx.extend(quantise_load(quarters[0], next_grouped, j))
         h_mx = []
         for i in range(GROUPS):
@@ -168,21 +170,27 @@ def tile_selsahead_pb_kernel(tc, h, w_q, b_q, w_k, b_k, out):
             h_mx.extend(quantise_rows(nc, keep, h_grouped, "h%d" % i))
 
         logits = []
+        late = []
         for step, (m, f_pass) in enumerate(quarters):
             last = step == len(quarters) - 1
             this_mx = next_mx
             next_mx = []
             lead = FIRST_LEAD if step == 0 else 0
-            products = [project(nc, sums_pool, this_mx, h_mx[i]) for i in range(lead)]
+            products = [project(nc, banks, this_mx, h_mx[i]) for i in range(lead)]
+            if not last:
+                next_grouped = transpose_quarter(quarters[step + 1])
+            products.extend([project(nc, banks, this_mx, h_mx[i]) for i in range(lead, GROUPS)])
             if last:
                 for i in range(GROUPS):
                     logits.append(banks.tile([P, PROPOSALS], F32, tag="bank", name="logits_%d" % i))
                     affinity_pass(logits[i], i, 0)
-            else:
-                next_grouped = transpose_quarter(quarters[step + 1])
-            products.extend([project(nc, sums_pool, this_mx, h_mx[i]) for i in range(lead, GROUPS)])
 
-            def finish_group(i):
+            rounded = [
+                keep.tile([P, P * PACK], BF16, name="rounded_%s%d_%d" % (m, f_pass, i), align_bytes=MX_ALIGN)
+                for i in range(GROUPS)
+            ]
+
+            def finish_group(i, m=m, f_pass=f_pass, last=last, rounded=rounded):
                 cols = slice(i * P, (i + 1) * P)
                 nc.vector.quantize_mx(
                     out=qk_codes[(m, f_pass)][:, cols].bitcast(FP8X4),
@@ -195,22 +203,35 @@ def tile_selsahead_pb_kernel(tc, h, w_q, b_q, w_k, b_k, out):
                     nc.scalar.mul(out=scaled[:], in_=logits[i][:], mul=SCALE)
                     nc.sync.dma_start(out=out[cols, :], in_=scaled[:])
 
-            rounded = []
-            for i in range(GROUPS):
-                j = i - lead
-                if not last and 0 <= j < LOADS:
-                    next_mx.extend(quantise_load(quarters[step + 1], next_grouped, j))
-                rounded.append(
-                    keep.tile(
-                        [P, P * PACK], BF16, name="rounded_%s%d_%d" % (m, f_pass, i), align_bytes=MX_ALIGN
+            on_scalar = SCALAR_GROUPS.get((m, f_pass), [])
+            on_vector = [i for i in range(GROUPS) if i not in on_scalar]
+            for i in on_scalar:
+                for t in range(PACK):
+                    nc.scalar.activation(
+                        out=rounded[i][:].rearrange("p (n t) -> p t n", t=PACK)[:, t],
+                        in_=products[i][:, t, :],
+                        func=mybir.ActivationFunctionType.Identity,
+                        bias=bias[m][:, f_pass, t : t + 1],
                     )
-                )
+            for n, i in enumerate(on_vector):
+                j = n - lead
+                if not last and 0 <= j < len(next_grouped):
+                    next_mx.extend(quantise_load(quarters[step + 1], next_grouped, j))
                 nc.vector.tensor_tensor(
                     out=rounded[i][:].rearrange("p (n t) -> p n t", t=PACK),
                     in0=products[i][:].rearrange("p t n -> p n t"),
                     in1=bias[m][:, f_pass, :].unsqueeze(1).to_broadcast([P, P, PACK]),
                     op=mybir.AluOpType.add,
                 )
-                if i >= 1:
-                    finish_group(i - 1)
-            finish_group(GROUPS - 1)
+                if n == 1:
+                    for finish in late:
+                        finish()
+                    late = []
+                if n >= 1:
+                    finish_group(on_vector[n - 1])
+            if last:
+                for i in on_scalar:
+                    finish_group(i)
+            else:
+                late = [functools.partial(finish_group, i) for i in on_scalar]
+            finish_group(on_vector[-1])

@@ -22,6 +22,7 @@ PAIRS = FEATURES // 2
 PAIRS_IN_WORD = PACK // 2
 TILE_WORDS = PASSES * P
 LOAD_ROWS = 2
+LOADS = PACK // LOAD_ROWS
 HEAD_LOAD_ROWS = 1
 SCALAR_GROUPS = {("k", 1): [1], ("q", 1): [1]}
 FIRST_LEAD = 2
@@ -32,7 +33,18 @@ SCALE = 1.0 / math.sqrt(FEATURES)
 FLOPS = 2 * 2 * PROPOSALS * FEATURES * FEATURES + 2 * PROPOSALS * PROPOSALS * FEATURES
 
 
-def transpose_rows(nc, banks, keep, raw, identity, label):
+def sort_pairs(copy, keep, raw, label):
+    count = raw[:].shape[1]
+    parted = keep.tile([P, count, FEATURES], BF16, name="parted_" + label)
+    for c in range(count):
+        copy(
+            out=parted[:, c, :].bitcast(F32).rearrange("p (g u r) -> p g u r", g=PASSES, u=PAIRS_IN_WORD),
+            in_=raw[:, c, :].bitcast(F32).rearrange("p (g r u) -> p g u r", g=PASSES, u=PAIRS_IN_WORD),
+        )
+    return parted
+
+
+def transpose_rows(nc, banks, keep, raw, identity, label, parted=False):
     count = raw[:].shape[1]
     grouped = keep.tile([P, count * FEATURES], BF16, name="grouped_" + label, align_bytes=MX_ALIGN)
     for c in range(count):
@@ -44,7 +56,9 @@ def transpose_rows(nc, banks, keep, raw, identity, label):
                 first = g * PAIRS_IN_WORD * P + u
                 nc.tensor.transpose(
                     turned[:, block * P : (block + 1) * P],
-                    pairs[:, first : (g + 1) * PAIRS_IN_WORD * P : PAIRS_IN_WORD],
+                    pairs[:, block * P : (block + 1) * P]
+                    if parted
+                    else pairs[:, first : (g + 1) * PAIRS_IN_WORD * P : PAIRS_IN_WORD],
                     identity[:],
                 )
         nc.scalar.copy(
@@ -118,12 +132,14 @@ def tile_selsahead_pb_kernel(tc, h, w_q, b_q, w_k, b_k, out):
                 loaded.append(raw)
             return loaded
 
-        w_raw = {quarters[0]: load_quarter(*quarters[0], HEAD_LOAD_ROWS)}
+        w_raw = {}
         h_raw = []
         for i in range(GROUPS):
             raw = keep.tile([P, 1, FEATURES], BF16, name="raw_h%d" % i)
             nc.sync.dma_start(out=raw[:, 0, :], in_=h[i * P : (i + 1) * P, :])
             h_raw.append(raw)
+            if i == 0:
+                w_raw[quarters[0]] = load_quarter(*quarters[0], HEAD_LOAD_ROWS)
         load_bias("k")
         load_bias("q")
         for quarter in quarters[1:]:
@@ -139,37 +155,56 @@ def tile_selsahead_pb_kernel(tc, h, w_q, b_q, w_k, b_k, out):
                 [P, PROPOSALS], U8, name="scales_%s%d" % (m, f_pass), align_bytes=MX_ALIGN
             )
 
+        parted = set()
+
+        def part(quarter, j, copy):
+            w_raw[quarter][j] = sort_pairs(copy, keep, w_raw[quarter][j], "%s%d_%d" % (quarter + (j,)))
+            parted.add((quarter, j))
+
         def transpose_quarter(quarter):
             return [
-                transpose_rows(nc, banks, keep, raw, identity, "%s%d_%d" % (quarter + (j,)))
+                transpose_rows(
+                    nc, banks, keep, raw, identity, "%s%d_%d" % (quarter + (j,)), (quarter, j) in parted
+                )
                 for j, raw in enumerate(w_raw[quarter])
             ]
 
         def quantise_load(quarter, quarter_grouped, j):
             return quantise_rows(nc, keep, quarter_grouped[j], "%s%d_%d" % (quarter + (j,)))
 
-        def affinity_pass(logits_i, i, f_pass):
-            cols = slice(i * P, (i + 1) * P)
-            nc.tensor.matmul_mx(
-                out=logits_i[:],
-                lhsT=qk_codes[("q", f_pass)][:, cols].bitcast(FP8X4),
-                lhsT_scale=qk_scales[("q", f_pass)][:, cols],
-                rhs=qk_codes[("k", f_pass)][:].bitcast(FP8X4),
-                rhs_scale=qk_scales[("k", f_pass)][:],
-                start=(f_pass == 0),
-                stop=(f_pass == PASSES - 1),
-            )
+        def affinity_pass(i, f_pass):
+            rows = slice(i * P, (i + 1) * P)
+            for cols, part_logits in logits[i]:
+                nc.tensor.matmul_mx(
+                    out=part_logits[:],
+                    lhsT=qk_codes[("q", f_pass)][:, rows].bitcast(FP8X4),
+                    lhsT_scale=qk_scales[("q", f_pass)][:, rows],
+                    rhs=qk_codes[("k", f_pass)][:, cols].bitcast(FP8X4),
+                    rhs_scale=qk_scales[("k", f_pass)][:, cols],
+                    start=(f_pass == 0),
+                    stop=(f_pass == PASSES - 1),
+                )
 
-        next_grouped = transpose_quarter(quarters[0])
-        next_mx = []
-        for j in range(len(next_grouped)):
-            next_mx.extend(quantise_load(quarters[0], next_grouped, j))
+        def store_logits(i):
+            for n, (cols, part_logits) in enumerate(logits[i]):
+                scaled = keep.tile([P, cols.stop - cols.start], F32, name="scaled_%d_%d" % (i, n))
+                if n == 0:
+                    nc.scalar.mul(out=scaled[:], in_=part_logits[:], mul=SCALE)
+                else:
+                    nc.vector.tensor_scalar_mul(out=scaled[:], in0=part_logits[:], scalar1=SCALE)
+                nc.sync.dma_start(out=out[i * P : (i + 1) * P, cols], in_=scaled[:])
+
         h_mx = []
         for i in range(GROUPS):
             h_grouped = transpose_rows(nc, banks, keep, h_raw[i], identity, "h%d" % i)
             h_mx.extend(quantise_rows(nc, keep, h_grouped, "h%d" % i))
+            if i == 0:
+                next_grouped = transpose_quarter(quarters[0])
+                next_mx = []
+                for j in range(len(next_grouped)):
+                    next_mx.extend(quantise_load(quarters[0], next_grouped, j))
 
-        logits = []
+        logits = {}
         late = []
         for step, (m, f_pass) in enumerate(quarters):
             last = step == len(quarters) - 1
@@ -179,12 +214,9 @@ def tile_selsahead_pb_kernel(tc, h, w_q, b_q, w_k, b_k, out):
             products = [project(nc, banks, this_mx, h_mx[i]) for i in range(lead)]
             if not last:
                 next_grouped = transpose_quarter(quarters[step + 1])
+            if step + 2 < len(quarters):
+                part(quarters[step + 2], LOADS - 1, nc.scalar.copy)
             products.extend([project(nc, banks, this_mx, h_mx[i]) for i in range(lead, GROUPS)])
-            if last:
-                for i in range(GROUPS):
-                    logits.append(banks.tile([P, PROPOSALS], F32, tag="bank", name="logits_%d" % i))
-                    affinity_pass(logits[i], i, 0)
-
             rounded = [
                 keep.tile([P, P * PACK], BF16, name="rounded_%s%d_%d" % (m, f_pass, i), align_bytes=MX_ALIGN)
                 for i in range(GROUPS)
@@ -198,10 +230,19 @@ def tile_selsahead_pb_kernel(tc, h, w_q, b_q, w_k, b_k, out):
                     in_=rounded[i][:],
                 )
                 if last:
-                    affinity_pass(logits[i], i, 1)
-                    scaled = keep.tile([P, PROPOSALS], F32, name="scaled_%d" % i)
-                    nc.scalar.mul(out=scaled[:], in_=logits[i][:], mul=SCALE)
-                    nc.sync.dma_start(out=out[cols, :], in_=scaled[:])
+                    affinity_pass(i, 1)
+                    store_logits(i)
+
+            def open_logits(i):
+                width = PROPOSALS // 2 if i == GROUPS - 1 else PROPOSALS
+                logits[i] = [
+                    (
+                        slice(first, first + width),
+                        banks.tile([P, width], F32, tag="bank", name="logits_%d_%d" % (i, first)),
+                    )
+                    for first in range(0, PROPOSALS, width)
+                ]
+                affinity_pass(i, 0)
 
             on_scalar = SCALAR_GROUPS.get((m, f_pass), [])
             on_vector = [i for i in range(GROUPS) if i not in on_scalar]
@@ -223,15 +264,19 @@ def tile_selsahead_pb_kernel(tc, h, w_q, b_q, w_k, b_k, out):
                     in1=bias[m][:, f_pass, :].unsqueeze(1).to_broadcast([P, P, PACK]),
                     op=mybir.AluOpType.add,
                 )
-                if n == 1:
-                    for finish in late:
-                        finish()
-                    late = []
-                if n >= 1:
-                    finish_group(on_vector[n - 1])
-            if last:
-                for i in on_scalar:
+                for finish in late:
+                    finish()
+                late = [functools.partial(finish_group, i)]
+                if last and n == 0:
+                    open_logits(i)
                     finish_group(i)
-            else:
-                late = [functools.partial(finish_group, i) for i in on_scalar]
-            finish_group(on_vector[-1])
+                    late = []
+                    for other in range(i + 1, GROUPS):
+                        open_logits(other)
+                if last and n == 1:
+                    for done in on_scalar + [i]:
+                        finish_group(done)
+                    late = []
+            for finish in late:
+                finish()
+            late = [functools.partial(finish_group, i) for i in on_scalar]

from contextlib import ExitStack
import functools
import math

import concourse.mybir as mybir
from concourse.masks import make_identity

F32 = mybir.dt.float32
BF16 = mybir.dt.bfloat16
U32 = mybir.dt.uint32
U8 = mybir.dt.uint8
FP8X4 = mybir.dt.float8_e4m3fn_x4

P = 128
PACK = 4
K_PASS = P * PACK
PROPOSALS = 512
FEATURES = 1024
PASSES = FEATURES // K_PASS
GROUPS = PROPOSALS // P
PAIRS = FEATURES // 2
PAIRS_IN_WORD = PACK // 2
TILE_WORDS = PASSES * P
LOAD_ROWS = 2
LOADS = PACK // LOAD_ROWS
HEAD_LOAD_ROWS = 1
SCALAR_GROUPS = {("k", 1): [1], ("q", 1): [1]}
FIRST_LEAD = 2
PSUM_BANKS = 8
MX_ALIGN = 64
SCALE = 1.0 / math.sqrt(FEATURES)

FLOPS = 2 * 2 * PROPOSALS * FEATURES * FEATURES + 2 * PROPOSALS * PROPOSALS * FEATURES


def sort_pairs(copy, keep, raw, label):
    count = raw[:].shape[1]
    parted = keep.tile([P, count, FEATURES], BF16, name="parted_" + label)
    for c in range(count):
        copy(
            out=parted[:, c, :].bitcast(F32).rearrange("p (g u r) -> p g u r", g=PASSES, u=PAIRS_IN_WORD),
            in_=raw[:, c, :].bitcast(F32).rearrange("p (g r u) -> p g u r", g=PASSES, u=PAIRS_IN_WORD),
        )
    return parted


def transpose_rows(nc, banks, keep, raw, identity, label, parted=False):
    count = raw[:].shape[1]
    grouped = keep.tile([P, count * FEATURES], BF16, name="grouped_" + label, align_bytes=MX_ALIGN)
    for c in range(count):
        pairs = raw[:, c, :].bitcast(F32)
        turned = banks.tile([P, PAIRS], F32, tag="bank")
        for g in range(PASSES):
            for u in range(PAIRS_IN_WORD):
                block = PAIRS_IN_WORD * g + u
                first = g * PAIRS_IN_WORD * P + u
                nc.tensor.transpose(
                    turned[:, block * P : (block + 1) * P],
                    pairs[:, block * P : (block + 1) * P]
                    if parted
                    else pairs[:, first : (g + 1) * PAIRS_IN_WORD * P : PAIRS_IN_WORD],
                    identity[:],
                )
        nc.scalar.copy(
            out=grouped[:, c * FEATURES : (c + 1) * FEATURES]
            .bitcast(F32)
            .rearrange("p (g r u) -> p g r u", g=PASSES, u=PAIRS_IN_WORD),
            in_=turned[:].rearrange("p (g u r) -> p g r u", g=PASSES, u=PAIRS_IN_WORD),
        )
    return grouped


def quantise_rows(nc, keep, grouped, label):
    width = grouped[:].shape[1] // PACK
    codes = keep.tile([P, width], U32, name="codes_" + label, align_bytes=MX_ALIGN)
    scales = keep.tile([P, width], U8, name="scales_" + label, align_bytes=MX_ALIGN)
    nc.vector.quantize_mx(out=codes[:].bitcast(FP8X4), scales=scales[:], in_=grouped[:])
    return [
        (codes[:, first : first + TILE_WORDS], scales[:, first : first + TILE_WORDS])
        for first in range(0, width, TILE_WORDS)
    ]


def project(nc, banks, weights, proposals):
    sums = banks.tile([P, PACK, P], F32, tag="bank")
    h_codes, h_scales = proposals
    for t in range(PACK):
        w_codes, w_scales = weights[t]
        for g in range(PASSES):
            cols = slice(g * P, (g + 1) * P)
            nc.tensor.matmul_mx(
                out=sums[:, t, :],
                lhsT=w_codes[:, cols].bitcast(FP8X4),
                lhsT_scale=w_scales[:, cols],
                rhs=h_codes[:, cols].bitcast(FP8X4),
                rhs_scale=h_scales[:, cols],
                start=(g == 0),
                stop=(g == PASSES - 1),
            )
    return sums


def tile_selsahead_pb_kernel(tc, h, w_q, b_q, w_k, b_k, out):
    nc = tc.nc
    weight_dram = {"q": w_q, "k": w_k}
    bias_dram = {"q": b_q, "k": b_k}
    quarters = [("k", 0), ("q", 0), ("k", 1), ("q", 1)]

    with ExitStack() as ctx:
        ctx.enter_context(tc.manual_schedule())
        keep = ctx.enter_context(tc.tile_pool(name="keep", bufs=1))
        banks = ctx.enter_context(tc.psum_pool(name="banks", bufs=PSUM_BANKS))

        identity = keep.tile([P, P], F32, name="identity")
        make_identity(nc, identity[:])

        bias = {}

        def load_bias(m):
            bias[m] = keep.tile([P, PASSES, PACK], BF16, name="bias_" + m)
            nc.sync.dma_start(
                out=bias[m][:],
                in_=bias_dram[m].rearrange("(g p t) -> p g t", g=PASSES, p=P, t=PACK),
            )

        def load_quarter(m, f_pass, load_rows):
            rows = weight_dram[m].rearrange("(g p t) d -> g p t d", g=PASSES, p=P, t=PACK)
            loaded = []
            for first in range(0, PACK, load_rows):
                raw = keep.tile([P, load_rows, FEATURES], BF16, name="raw_%s%d_%d" % (m, f_pass, first))
                nc.sync.dma_start(out=raw[:], in_=rows[f_pass, :, first : first + load_rows, :])
                loaded.append(raw)
            return loaded

        w_raw = {}
        h_raw = []
        for i in range(GROUPS):
            raw = keep.tile([P, 1, FEATURES], BF16, name="raw_h%d" % i)
            nc.sync.dma_start(out=raw[:, 0, :], in_=h[i * P : (i + 1) * P, :])
            h_raw.append(raw)
            if i == 0:
                w_raw[quarters[0]] = load_quarter(*quarters[0], HEAD_LOAD_ROWS)
        load_bias("k")
        load_bias("q")
        for quarter in quarters[1:]:
            w_raw[quarter] = load_quarter(*quarter, LOAD_ROWS)

        qk_codes = {}
        qk_scales = {}
        for m, f_pass in quarters:
            qk_codes[(m, f_pass)] = keep.tile(
                [P, PROPOSALS], U32, name="codes_%s%d" % (m, f_pass), align_bytes=MX_ALIGN
            )
            qk_scales[(m, f_pass)] = keep.tile(
                [P, PROPOSALS], U8, name="scales_%s%d" % (m, f_pass), align_bytes=MX_ALIGN
            )

        parted = set()

        def part(quarter, j, copy):
            w_raw[quarter][j] = sort_pairs(copy, keep, w_raw[quarter][j], "%s%d_%d" % (quarter + (j,)))
            parted.add((quarter, j))

        def transpose_quarter(quarter):
            return [
                transpose_rows(
                    nc, banks, keep, raw, identity, "%s%d_%d" % (quarter + (j,)), (quarter, j) in parted
                )
                for j, raw in enumerate(w_raw[quarter])
            ]

        def quantise_load(quarter, quarter_grouped, j):
            return quantise_rows(nc, keep, quarter_grouped[j], "%s%d_%d" % (quarter + (j,)))

        def affinity_pass(i, f_pass):
            rows = slice(i * P, (i + 1) * P)
            for cols, part_logits in logits[i]:
                nc.tensor.matmul_mx(
                    out=part_logits[:],
                    lhsT=qk_codes[("q", f_pass)][:, rows].bitcast(FP8X4),
                    lhsT_scale=qk_scales[("q", f_pass)][:, rows],
                    rhs=qk_codes[("k", f_pass)][:, cols].bitcast(FP8X4),
                    rhs_scale=qk_scales[("k", f_pass)][:, cols],
                    start=(f_pass == 0),
                    stop=(f_pass == PASSES - 1),
                )

        def store_logits(i):
            for n, (cols, part_logits) in enumerate(logits[i]):
                scaled = keep.tile([P, cols.stop - cols.start], F32, name="scaled_%d_%d" % (i, n))
                if n == 0:
                    nc.scalar.mul(out=scaled[:], in_=part_logits[:], mul=SCALE)
                else:
                    nc.vector.tensor_scalar_mul(out=scaled[:], in0=part_logits[:], scalar1=SCALE)
                nc.sync.dma_start(out=out[i * P : (i + 1) * P, cols], in_=scaled[:])

        h_mx = []
        for i in range(GROUPS):
            h_grouped = transpose_rows(nc, banks, keep, h_raw[i], identity, "h%d" % i)
            h_mx.extend(quantise_rows(nc, keep, h_grouped, "h%d" % i))
            if i == 0:
                next_grouped = transpose_quarter(quarters[0])
                next_mx = []
                for j in range(len(next_grouped)):
                    next_mx.extend(quantise_load(quarters[0], next_grouped, j))

        logits = {}
        late = []
        for step, (m, f_pass) in enumerate(quarters):
            last = step == len(quarters) - 1
            this_mx = next_mx
            next_mx = []
            lead = FIRST_LEAD if step == 0 else 0
            products = [project(nc, banks, this_mx, h_mx[i]) for i in range(lead)]
            if not last:
                next_grouped = transpose_quarter(quarters[step + 1])
            if step + 2 < len(quarters):
                part(quarters[step + 2], LOADS - 1, nc.scalar.copy)
            products.extend([project(nc, banks, this_mx, h_mx[i]) for i in range(lead, GROUPS)])
            rounded = [
                keep.tile([P, P * PACK], BF16, name="rounded_%s%d_%d" % (m, f_pass, i), align_bytes=MX_ALIGN)
                for i in range(GROUPS)
            ]

            def finish_group(i, m=m, f_pass=f_pass, last=last, rounded=rounded):
                cols = slice(i * P, (i + 1) * P)
                nc.vector.quantize_mx(
                    out=qk_codes[(m, f_pass)][:, cols].bitcast(FP8X4),
                    scales=qk_scales[(m, f_pass)][:, cols],
                    in_=rounded[i][:],
                )
                if last:
                    affinity_pass(i, 1)
                    store_logits(i)

            def open_logits(i):
                width = PROPOSALS // 2 if i == GROUPS - 1 else PROPOSALS
                logits[i] = [
                    (
                        slice(first, first + width),
                        banks.tile([P, width], F32, tag="bank", name="logits_%d_%d" % (i, first)),
                    )
                    for first in range(0, PROPOSALS, width)
                ]
                affinity_pass(i, 0)

            on_scalar = SCALAR_GROUPS.get((m, f_pass), [])
            on_vector = [i for i in range(GROUPS) if i not in on_scalar]
            for i in on_scalar:
                for t in range(PACK):
                    nc.scalar.activation(
                        out=rounded[i][:].rearrange("p (n t) -> p t n", t=PACK)[:, t],
                        in_=products[i][:, t, :],
                        func=mybir.ActivationFunctionType.Identity,
                        bias=bias[m][:, f_pass, t : t + 1],
                    )
            for n, i in enumerate(on_vector):
                j = n - lead
                if not last and 0 <= j < len(next_grouped):
                    next_mx.extend(quantise_load(quarters[step + 1], next_grouped, j))
                nc.vector.tensor_tensor(
                    out=rounded[i][:].rearrange("p (n t) -> p n t", t=PACK),
                    in0=products[i][:].rearrange("p t n -> p n t"),
                    in1=bias[m][:, f_pass, :].unsqueeze(1).to_broadcast([P, P, PACK]),
                    op=mybir.AluOpType.add,
                )
                for finish in late:
                    finish()
                late = [functools.partial(finish_group, i)]
                if last and n == 0:
                    open_logits(i)
                    finish_group(i)
                    late = []
                    for other in range(i + 1, GROUPS):
                        open_logits(other)
                if last and n == 1:
                    for done in on_scalar + [i]:
                        finish_group(done)
                    late = []
            for finish in late:
                finish()
            late = [functools.partial(finish_group, i) for i in on_scalar]
